import numpy as np
import ml_dtypes


def mxq(x, axis, fmt="e4m3"):
    dtype, down = {"e4m3": (ml_dtypes.float8_e4m3fn, 7), "e5m2": (ml_dtypes.float8_e5m2, 14)}[fmt]
    v = np.moveaxis(np.asarray(x, np.float32).astype(ml_dtypes.bfloat16).astype(np.float64), axis, -1)
    blocks = v.reshape(v.shape[:-1] + (-1, 32))
    amax = np.abs(blocks).max(-1, keepdims=True)
    byte = np.maximum(np.where(amax > 0, np.frexp(amax)[1] - 1 + 127, 0) - down, 1)
    scale = np.exp2(byte - 127.0)
    codes = (blocks / scale).astype(np.float32).astype(dtype).astype(np.float64)
    return np.moveaxis((codes * scale).reshape(v.shape), -1, axis)


WIDE = False


def mx_kscale(k):
    if not WIDE:
        return np.ones(k)
    levels = np.array([10, -10, 5, -5, 0])
    a = np.random.permutation(np.resize(levels, k // 512 * 4)).reshape(k // 512, 4)
    idx = np.arange(k)
    return np.exp2(a[idx // 512, idx % 128 // 32])


BF16 = ml_dtypes.bfloat16


def bf(x):
    return np.asarray(x, np.float32).astype(BF16)


def f64(x):
    return np.asarray(x).astype(np.float64)


N, C, D, H, W = 2, 8, 512, 4, 4
EPS = 1e-5


def setup_inputs():
    t = np.minimum(mx_kscale(D), 1.0) ** 2
    sig0 = 0.01 * (0.5 + np.random.random_sample((C, D)))
    sig = sig0 * t
    r = np.exp2(np.round(np.log2((sig / np.sqrt(sig**2 + EPS)) / (sig0 / np.sqrt(sig0**2 + EPS)))))
    mu = np.random.standard_normal((C, D))
    z = np.random.standard_normal((N, C, D, H, W))
    x = ((z + mu[None, :, :, None, None]) * sig[None, :, :, None, None]).reshape(N, C * D, H, W)
    weight = (np.eye(D)[None] + np.random.standard_normal((C, D, D)) / np.sqrt(D)) / r[:, None, :]
    return {"x": bf(x), "weight": bf(weight), "bias": bf(np.random.standard_normal(C * D) * 0.3)}


def reference(x, weight, bias):
    x, weight, bias = f64(x), f64(weight), f64(bias)
    n, cd, h, w = x.shape
    c = weight.shape[0]
    d = cd // c
    mean = np.mean(x, axis=(0, 2, 3), keepdims=True)
    var = np.mean(np.square(x - mean), axis=(0, 2, 3), keepdims=True)
    xn = (x - mean) / np.sqrt(var + EPS)
    xg = xn.reshape(n, c, d, h * w)
    out = mxq(weight, 2, "e4m3")[None] @ mxq(xg, 2, "e4m3")
    return out.reshape(n, cd, h, w) + bias[None, :, None, None]

@@ -1,0 +1,190 @@
+from contextlib import ExitStack
+
+import concourse.mybir as mybir
+from concourse.masks import make_identity
+
+F32 = mybir.dt.float32
+BF16 = mybir.dt.bfloat16
+U32 = mybir.dt.uint32
+U8 = mybir.dt.uint8
+FP8X4 = mybir.dt.float8_e4m3fn_x4
+ALU = mybir.AluOpType
+ACT = mybir.ActivationFunctionType
+AXIS = mybir.AxisListType
+
+P = 128
+PACK = 4
+BATCH = 2
+CAPS = 8
+D = 512
+HW = 16
+EPS = 1e-5
+SAMPLES = BATCH * HW
+O_TILES = D // P
+GROUPS = 2
+GROUP_CAPS = CAPS // GROUPS
+GROUP_CH = GROUP_CAPS * PACK
+BANK_TILES = 2
+
+FLOPS = 2 * CAPS * D * D * SAMPLES
+
+
+def normalise_and_quantise(nc, pool, x_group):
+    total = pool.tile([P, GROUP_CH], F32)
+    nc.vector.tensor_reduce(
+        out=total[:],
+        in_=x_group[:].rearrange("q n c t s -> q (c t) n s"),
+        axis=AXIS.XY,
+        op=ALU.add,
+    )
+    neg_mean = pool.tile([P, GROUP_CH], F32)
+    nc.vector.tensor_scalar_mul(out=neg_mean[:], in0=total[:], scalar1=-1.0 / SAMPLES)
+    centred = pool.tile([P, BATCH, GROUP_CH, HW], F32)
+    nc.vector.tensor_tensor(
+        out=centred[:],
+        in0=x_group[:].rearrange("q n c t s -> q n (c t) s"),
+        in1=neg_mean[:].unsqueeze(1).unsqueeze(3).to_broadcast([P, BATCH, GROUP_CH, HW]),
+        op=ALU.add,
+    )
+    squared = pool.tile([P, BATCH, GROUP_CH, HW], F32)
+    nc.scalar.activation(out=squared[:], in_=centred[:], func=ACT.Square)
+    sum_sq = pool.tile([P, GROUP_CH], F32)
+    nc.vector.tensor_reduce(
+        out=sum_sq[:],
+        in_=squared[:].rearrange("q n k s -> q k n s"),
+        axis=AXIS.XY,
+        op=ALU.add,
+    )
+    var_eps = pool.tile([P, GROUP_CH], F32)
+    nc.vector.tensor_scalar(
+        out=var_eps[:],
+        in0=sum_sq[:],
+        scalar1=1.0 / SAMPLES,
+        scalar2=EPS,
+        op0=ALU.mult,
+        op1=ALU.add,
+    )
+    std = pool.tile([P, GROUP_CH], F32)
+    nc.scalar.activation(out=std[:], in_=var_eps[:], func=ACT.Sqrt)
+    rstd = pool.tile([P, GROUP_CH], F32)
+    nc.vector.reciprocal(out=rstd[:], in_=std[:])
+
+    xn = pool.tile([P, BATCH, GROUP_CAPS, HW, PACK], BF16, align_bytes=64)
+    for n in range(BATCH):
+        nc.vector.tensor_tensor(
+            out=xn[:, n],
+            in0=centred[:, n].rearrange("q (c t) s -> q c s t", t=PACK),
+            in1=rstd[:]
+            .rearrange("q (c t) -> q c t", t=PACK)
+            .unsqueeze(2)
+            .to_broadcast([P, GROUP_CAPS, HW, PACK]),
+            op=ALU.mult,
+        )
+    x_codes = pool.tile([P, GROUP_CAPS * SAMPLES], U32, align_bytes=64)
+    x_scales = pool.tile([P, GROUP_CAPS * SAMPLES], U8, align_bytes=64)
+    nc.vector.quantize_mx(
+        out=x_codes[:].bitcast(FP8X4),
+        scales=x_scales[:],
+        in_=xn[:].rearrange("q n c s t -> q (n c s t)"),
+    )
+    return x_codes, x_scales
+
+
+def tile_caps_bn_s_kernel(tc, x, weight, bias, out):
+    nc = tc.nc
+    with ExitStack() as ctx:
+        consts = ctx.enter_context(tc.tile_pool(name="consts", bufs=1))
+        acts = ctx.enter_context(tc.tile_pool(name="acts", bufs=GROUPS))
+        caps = ctx.enter_context(tc.tile_pool(name="caps", bufs=CAPS))
+        turned_pool = ctx.enter_context(tc.psum_pool(name="turned", bufs=6))
+        product_pool = ctx.enter_context(tc.psum_pool(name="product", bufs=2))
+
+        x_view = x.rearrange(
+            "n (c u q e) h w -> q n c u (e h w)", c=CAPS, u=2, q=P, e=2
+        )
+        x_groups = []
+        for g in range(GROUPS):
+            x_group = acts.tile([P, BATCH, GROUP_CAPS, PACK, HW], BF16)
+            for n in range(BATCH):
+                nc.sync.dma_start(
+                    out=x_group[:, n].rearrange("q c (u e) s -> q c u (e s)", u=2),
+                    in_=x_view[:, n, g * GROUP_CAPS : (g + 1) * GROUP_CAPS],
+                )
+            x_groups.append(x_group)
+        bias_sb = consts.tile([P, CAPS, O_TILES], BF16)
+        nc.scalar.dma_start(
+            out=bias_sb[:], in_=bias.rearrange("(c p j) -> p c j", c=CAPS, p=P)
+        )
+        w_rows_all = []
+        for c in range(CAPS):
+            w_rows = caps.tile([P, O_TILES, D], BF16)
+            nc.sync.dma_start(
+                out=w_rows[:], in_=weight[c].rearrange("(p j) i -> p j i", j=O_TILES)
+            )
+            w_rows_all.append(w_rows)
+
+        ident = consts.tile([P, P], F32)
+        make_identity(nc, ident[:])
+        ones = consts.tile([P, 1], F32)
+        nc.vector.memset(ones[:], 1.0)
+        table_warmer = consts.tile([P, 1], F32)
+        nc.scalar.activation(out=table_warmer[:], in_=ones[:], func=ACT.Sqrt)
+
+        x_mx = [normalise_and_quantise(nc, acts, x_groups[g]) for g in range(GROUPS)]
+
+        out_view = out.rearrange(
+            "n (c p j) h w -> c p n (j h w)", c=CAPS, p=P, j=O_TILES
+        )
+        for c in range(CAPS):
+            w_words = w_rows_all[c][:].bitcast(F32)
+            grouped = caps.tile([P, O_TILES, P, PACK], BF16, align_bytes=64)
+            grouped_words = grouped[:].bitcast(F32)
+            w_codes = caps.tile([P, O_TILES * P], U32, align_bytes=64)
+            w_scales = caps.tile([P, O_TILES * P], U8, align_bytes=64)
+            for j0 in range(0, O_TILES, BANK_TILES):
+                turned = turned_pool.tile([P, BANK_TILES, 2, P], F32)
+                for jj in range(BANK_TILES):
+                    for u in range(2):
+                        nc.tensor.transpose(
+                            turned[:, jj, u, :],
+                            w_words[:, j0 + jj, u * P : (u + 1) * P],
+                            ident[:],
+                        )
+                nc.scalar.copy(
+                    out=grouped_words[:, j0 : j0 + BANK_TILES],
+                    in_=turned[:].rearrange("q j u r -> q j r u"),
+                )
+                cols = slice(j0 * P, (j0 + BANK_TILES) * P)
+                nc.vector.quantize_mx(
+                    out=w_codes[:, cols].bitcast(FP8X4),
+                    scales=w_scales[:, cols],
+                    in_=grouped[:, j0 : j0 + BANK_TILES].rearrange("q j r t -> q (j r t)"),
+                )
+
+            x_codes, x_scales = x_mx[c // GROUP_CAPS]
+            product = product_pool.tile([P, O_TILES, GROUP_CAPS * SAMPLES], F32)
+            for j in range(O_TILES):
+                nc.tensor.matmul_mx(
+                    out=product[:, j, :],
+                    lhsT=w_codes[:, j * P : (j + 1) * P].bitcast(FP8X4),
+                    lhsT_scale=w_scales[:, j * P : (j + 1) * P],
+                    rhs=x_codes[:].bitcast(FP8X4),
+                    rhs_scale=x_scales[:],
+                    start=True,
+                    stop=True,
+                )
+            result = caps.tile([P, BATCH, O_TILES, HW], F32)
+            nc.vector.tensor_tensor(
+                out=result[:],
+                in0=product[:].rearrange(
+                    "p j (n c s) -> p c n j s", n=BATCH, c=GROUP_CAPS
+                )[:, c % GROUP_CAPS],
+                in1=bias_sb[:, c, :]
+                .unsqueeze(1)
+                .unsqueeze(3)
+                .to_broadcast([P, BATCH, O_TILES, HW]),
+                op=ALU.add,
+            )
+            nc.sync.dma_start(
+                out=out_view[c], in_=result[:].rearrange("p n j s -> p n (j s)")
+            )

@@ -29,7 +29,10 @@ BANK_TILES = 2
 FLOPS = 2 * CAPS * D * D * SAMPLES
 
 
-def normalise_and_quantise(nc, pool, x_group):
+LAG = 3
+
+
+def centre(nc, pool, x_group):
     total = pool.tile([P, GROUP_CH], F32)
     nc.vector.tensor_reduce(
         out=total[:],
@@ -46,8 +49,16 @@ def normalise_and_quantise(nc, pool, x_group):
         in1=neg_mean[:].unsqueeze(1).unsqueeze(3).to_broadcast([P, BATCH, GROUP_CH, HW]),
         op=ALU.add,
     )
+    return centred
+
+
+def square(nc, pool, centred):
     squared = pool.tile([P, BATCH, GROUP_CH, HW], F32)
     nc.scalar.activation(out=squared[:], in_=centred[:], func=ACT.Square)
+    return squared
+
+
+def deviation(nc, pool, squared):
     sum_sq = pool.tile([P, GROUP_CH], F32)
     nc.vector.tensor_reduce(
         out=sum_sq[:],
@@ -66,9 +77,12 @@ def normalise_and_quantise(nc, pool, x_group):
     )
     std = pool.tile([P, GROUP_CH], F32)
     nc.scalar.activation(out=std[:], in_=var_eps[:], func=ACT.Sqrt)
+    return std
+
+
+def normalise(nc, pool, centred, std):
     rstd = pool.tile([P, GROUP_CH], F32)
     nc.vector.reciprocal(out=rstd[:], in_=std[:])
-
     xn = pool.tile([P, BATCH, GROUP_CAPS, HW, PACK], BF16, align_bytes=64)
     for n in range(BATCH):
         nc.vector.tensor_tensor(
@@ -80,6 +94,10 @@ def normalise_and_quantise(nc, pool, x_group):
             .to_broadcast([P, GROUP_CAPS, HW, PACK]),
             op=ALU.mult,
         )
+    return xn
+
+
+def quantise_samples(nc, pool, xn):
     x_codes = pool.tile([P, GROUP_CAPS * SAMPLES], U32, align_bytes=64)
     x_scales = pool.tile([P, GROUP_CAPS * SAMPLES], U8, align_bytes=64)
     nc.vector.quantize_mx(
@@ -90,6 +108,61 @@ def normalise_and_quantise(nc, pool, x_group):
     return x_codes, x_scales
 
 
+def turn_weights(nc, pool, turned_pool, w_rows, ident):
+    w_words = w_rows[:].bitcast(F32)
+    grouped = pool.tile([P, O_TILES, P, PACK], BF16, align_bytes=64)
+    grouped_words = grouped[:].bitcast(F32)
+    for j0 in range(0, O_TILES, BANK_TILES):
+        turned = turned_pool.tile([P, BANK_TILES, 2, P], F32)
+        for jj in range(BANK_TILES):
+            for u in range(2):
+                nc.tensor.transpose(
+                    turned[:, jj, u, :], w_words[:, j0 + jj, u * P : (u + 1) * P], ident[:]
+                )
+        nc.scalar.copy(
+            out=grouped_words[:, j0 : j0 + BANK_TILES],
+            in_=turned[:].rearrange("q j u r -> q j r u"),
+        )
+    return grouped
+
+
+def quantise_weights(nc, pool, grouped):
+    w_codes = pool.tile([P, O_TILES * P], U32, align_bytes=64)
+    w_scales = pool.tile([P, O_TILES * P], U8, align_bytes=64)
+    for j0 in range(0, O_TILES, BANK_TILES):
+        cols = slice(j0 * P, (j0 + BANK_TILES) * P)
+        nc.vector.quantize_mx(
+            out=w_codes[:, cols].bitcast(FP8X4),
+            scales=w_scales[:, cols],
+            in_=grouped[:, j0 : j0 + BANK_TILES].rearrange("q j r t -> q (j r t)"),
+        )
+    return w_codes, w_scales
+
+
+def multiply(nc, pool, product_pool, w_mx, x_mx, place, bias_c, out_c):
+    w_codes, w_scales = w_mx
+    x_codes, x_scales = x_mx
+    product = product_pool.tile([P, O_TILES, GROUP_CAPS * SAMPLES], F32)
+    for j in range(O_TILES):
+        nc.tensor.matmul_mx(
+            out=product[:, j, :],
+            lhsT=w_codes[:, j * P : (j + 1) * P].bitcast(FP8X4),
+            lhsT_scale=w_scales[:, j * P : (j + 1) * P],
+            rhs=x_codes[:].bitcast(FP8X4),
+            rhs_scale=x_scales[:],
+            start=True,
+            stop=True,
+        )
+    result = pool.tile([P, BATCH, O_TILES, HW], F32)
+    nc.vector.tensor_tensor(
+        out=result[:],
+        in0=product[:].rearrange("p j (n c s) -> p c n j s", n=BATCH, c=GROUP_CAPS)[:, place],
+        in1=bias_c.unsqueeze(1).unsqueeze(3).to_broadcast([P, BATCH, O_TILES, HW]),
+        op=ALU.add,
+    )
+    nc.sync.dma_start(out=out_c, in_=result[:].rearrange("p n j s -> p n (j s)"))
+
+
 def tile_caps_bn_s_kernel(tc, x, weight, bias, out):
     nc = tc.nc
     with ExitStack() as ctx:
@@ -98,6 +171,7 @@ def tile_caps_bn_s_kernel(tc, x, weight, bias, out):
         caps = ctx.enter_context(tc.tile_pool(name="caps", bufs=CAPS))
         turned_pool = ctx.enter_context(tc.psum_pool(name="turned", bufs=6))
         product_pool = ctx.enter_context(tc.psum_pool(name="product", bufs=2))
+        ctx.enter_context(tc.manual_schedule())
 
         x_view = x.rearrange(
             "n (c u q e) h w -> q n c u (e h w)", c=CAPS, u=2, q=P, e=2
@@ -130,61 +204,31 @@ def tile_caps_bn_s_kernel(tc, x, weight, bias, out):
         table_warmer = consts.tile([P, 1], F32)
         nc.scalar.activation(out=table_warmer[:], in_=ones[:], func=ACT.Sqrt)
 
-        x_mx = [normalise_and_quantise(nc, acts, x_groups[g]) for g in range(GROUPS)]
+        groups = range(GROUPS)
+        centred = [centre(nc, acts, x_groups[g]) for g in groups]
+        squared = [square(nc, acts, centred[g]) for g in groups]
+        grouped_0 = turn_weights(nc, caps, turned_pool, w_rows_all[0], ident)
+        std = [deviation(nc, acts, squared[g]) for g in groups]
+        w_mx = [quantise_weights(nc, caps, grouped_0)]
+        xn = [normalise(nc, acts, centred[g], std[g]) for g in groups]
+        x_mx = [quantise_samples(nc, acts, xn[g]) for g in groups]
 
         out_view = out.rearrange(
             "n (c p j) h w -> c p n (j h w)", c=CAPS, p=P, j=O_TILES
         )
-        for c in range(CAPS):
-            w_words = w_rows_all[c][:].bitcast(F32)
-            grouped = caps.tile([P, O_TILES, P, PACK], BF16, align_bytes=64)
-            grouped_words = grouped[:].bitcast(F32)
-            w_codes = caps.tile([P, O_TILES * P], U32, align_bytes=64)
-            w_scales = caps.tile([P, O_TILES * P], U8, align_bytes=64)
-            for j0 in range(0, O_TILES, BANK_TILES):
-                turned = turned_pool.tile([P, BANK_TILES, 2, P], F32)
-                for jj in range(BANK_TILES):
-                    for u in range(2):
-                        nc.tensor.transpose(
-                            turned[:, jj, u, :],
-                            w_words[:, j0 + jj, u * P : (u + 1) * P],
-                            ident[:],
-                        )
-                nc.scalar.copy(
-                    out=grouped_words[:, j0 : j0 + BANK_TILES],
-                    in_=turned[:].rearrange("q j u r -> q j r u"),
+        for c in range(1, CAPS + LAG):
+            if c < CAPS:
+                grouped = turn_weights(nc, caps, turned_pool, w_rows_all[c], ident)
+                w_mx.append(quantise_weights(nc, caps, grouped))
+            if c >= LAG:
+                m = c - LAG
+                multiply(
+                    nc,
+                    caps,
+                    product_pool,
+                    w_mx[m],
+                    x_mx[m // GROUP_CAPS],
+                    m % GROUP_CAPS,
+                    bias_sb[:, m, :],
+                    out_view[m],
                 )
-                cols = slice(j0 * P, (j0 + BANK_TILES) * P)
-                nc.vector.quantize_mx(
-                    out=w_codes[:, cols].bitcast(FP8X4),
-                    scales=w_scales[:, cols],
-                    in_=grouped[:, j0 : j0 + BANK_TILES].rearrange("q j r t -> q (j r t)"),
-                )
-
-            x_codes, x_scales = x_mx[c // GROUP_CAPS]
-            product = product_pool.tile([P, O_TILES, GROUP_CAPS * SAMPLES], F32)
-            for j in range(O_TILES):
-                nc.tensor.matmul_mx(
-                    out=product[:, j, :],
-                    lhsT=w_codes[:, j * P : (j + 1) * P].bitcast(FP8X4),
-                    lhsT_scale=w_scales[:, j * P : (j + 1) * P],
-                    rhs=x_codes[:].bitcast(FP8X4),
-                    rhs_scale=x_scales[:],
-                    start=True,
-                    stop=True,
-                )
-            result = caps.tile([P, BATCH, O_TILES, HW], F32)
-            nc.vector.tensor_tensor(
-                out=result[:],
-                in0=product[:].rearrange(
-                    "p j (n c s) -> p c n j s", n=BATCH, c=GROUP_CAPS
-                )[:, c % GROUP_CAPS],
-                in1=bias_sb[:, c, :]
-                .unsqueeze(1)
-                .unsqueeze(3)
-                .to_broadcast([P, BATCH, O_TILES, HW]),
-                op=ALU.add,
-            )
-            nc.sync.dma_start(
-                out=out_view[c], in_=result[:].rearrange("p n j s -> p n (j s)")
-            )

@@ -7,6 +7,7 @@ F32 = mybir.dt.float32
 BF16 = mybir.dt.bfloat16
 U32 = mybir.dt.uint32
 U8 = mybir.dt.uint8
+I32 = mybir.dt.int32
 FP8X4 = mybir.dt.float8_e4m3fn_x4
 ALU = mybir.AluOpType
 ACT = mybir.ActivationFunctionType
@@ -30,24 +31,29 @@ FLOPS = 2 * CAPS * D * D * SAMPLES
 
 
 LAG = 3
+IDLE_COLS = 512
+IDLE_FIRST = 12
 
 
-def centre(nc, pool, x_group):
-    total = pool.tile([P, GROUP_CH], F32)
+def channel_sums(nc, pool, values):
+    sums = pool.tile([P, GROUP_CH], F32)
     nc.vector.tensor_reduce(
-        out=total[:],
-        in_=x_group[:].rearrange("q n c t s -> q (c t) n s"),
-        axis=AXIS.XY,
-        op=ALU.add,
+        out=sums[:], in_=values.rearrange("q n k s -> q k n s"), axis=AXIS.XY, op=ALU.add
     )
+    return sums
+
+
+def over_samples(per_channel):
+    return per_channel[:].unsqueeze(1).unsqueeze(3).to_broadcast([P, BATCH, GROUP_CH, HW])
+
+
+def centre(nc, pool, x_values):
+    total = channel_sums(nc, pool, x_values)
     neg_mean = pool.tile([P, GROUP_CH], F32)
     nc.vector.tensor_scalar_mul(out=neg_mean[:], in0=total[:], scalar1=-1.0 / SAMPLES)
     centred = pool.tile([P, BATCH, GROUP_CH, HW], F32)
     nc.vector.tensor_tensor(
-        out=centred[:],
-        in0=x_group[:].rearrange("q n c t s -> q n (c t) s"),
-        in1=neg_mean[:].unsqueeze(1).unsqueeze(3).to_broadcast([P, BATCH, GROUP_CH, HW]),
-        op=ALU.add,
+        out=centred[:], in0=x_values, in1=over_samples(neg_mean), op=ALU.add
     )
     return centred
 
@@ -58,14 +64,7 @@ def square(nc, pool, centred):
     return squared
 
 
-def deviation(nc, pool, squared):
-    sum_sq = pool.tile([P, GROUP_CH], F32)
-    nc.vector.tensor_reduce(
-        out=sum_sq[:],
-        in_=squared[:].rearrange("q n k s -> q k n s"),
-        axis=AXIS.XY,
-        op=ALU.add,
-    )
+def deviation(nc, pool, sum_sq):
     var_eps = pool.tile([P, GROUP_CH], F32)
     nc.vector.tensor_scalar(
         out=var_eps[:],
@@ -80,9 +79,13 @@ def deviation(nc, pool, squared):
     return std
 
 
-def normalise(nc, pool, centred, std):
+def reciprocal(nc, pool, std):
     rstd = pool.tile([P, GROUP_CH], F32)
     nc.vector.reciprocal(out=rstd[:], in_=std[:])
+    return rstd
+
+
+def normalise(nc, pool, centred, rstd):
     xn = pool.tile([P, BATCH, GROUP_CAPS, HW, PACK], BF16, align_bytes=64)
     for n in range(BATCH):
         nc.vector.tensor_tensor(
@@ -163,6 +166,18 @@ def multiply(nc, pool, product_pool, w_mx, x_mx, place, bias_c, out_c):
     nc.sync.dma_start(out=out_c, in_=result[:].rearrange("p n j s -> p n (j s)"))
 
 
+def idle_pass(nc, idle_sum, zero_codes, zero_scales, k):
+    nc.tensor.matmul_mx(
+        out=idle_sum[:],
+        lhsT=zero_codes[:, 0:P].bitcast(FP8X4),
+        lhsT_scale=zero_scales[:, 0:P],
+        rhs=zero_codes[:].bitcast(FP8X4),
+        rhs_scale=zero_scales[:],
+        start=(k == 0),
+        stop=(k == IDLE_FIRST + LAG - 1),
+    )
+
+
 def tile_caps_bn_s_kernel(tc, x, weight, bias, out):
     nc = tc.nc
     with ExitStack() as ctx:
@@ -185,18 +200,31 @@ def tile_caps_bn_s_kernel(tc, x, weight, bias, out):
                     in_=x_view[:, n, g * GROUP_CAPS : (g + 1) * GROUP_CAPS],
                 )
             x_groups.append(x_group)
-        bias_sb = consts.tile([P, CAPS, O_TILES], BF16)
-        nc.scalar.dma_start(
-            out=bias_sb[:], in_=bias.rearrange("(c p j) -> p c j", c=CAPS, p=P)
-        )
         w_rows_all = []
         for c in range(CAPS):
             w_rows = caps.tile([P, O_TILES, D], BF16)
-            nc.sync.dma_start(
-                out=w_rows[:], in_=weight[c].rearrange("(p j) i -> p j i", j=O_TILES)
-            )
+            w_view = weight[c].rearrange("(p j) i -> p j i", j=O_TILES)
+            if c < CAPS - 1:
+                nc.sync.dma_start(out=w_rows[:], in_=w_view)
+            else:
+                for j0 in range(0, O_TILES, BANK_TILES):
+                    nc.sync.dma_start(
+                        out=w_rows[:, j0 : j0 + BANK_TILES], in_=w_view[:, j0 : j0 + BANK_TILES]
+                    )
             w_rows_all.append(w_rows)
 
+        bias_rows = consts.tile([P, D], BF16)
+        nc.vector.memset(bias_rows[:].bitcast(I32), 0)
+        nc.scalar.dma_start(
+            out=bias_rows[0:CAPS, :], in_=bias.rearrange("(c o) -> c o", c=CAPS)
+        )
+        zeros = consts.tile([P, IDLE_COLS * PACK], BF16, align_bytes=64)
+        nc.vector.memset(zeros[:].bitcast(I32), 0)
+        zero_codes = consts.tile([P, IDLE_COLS], U32, align_bytes=64)
+        zero_scales = consts.tile([P, IDLE_COLS], U8, align_bytes=64)
+        nc.vector.quantize_mx(
+            out=zero_codes[:].bitcast(FP8X4), scales=zero_scales[:], in_=zeros[:]
+        )
         ident = consts.tile([P, P], F32)
         make_identity(nc, ident[:])
         ones = consts.tile([P, 1], F32)
@@ -204,13 +232,33 @@ def tile_caps_bn_s_kernel(tc, x, weight, bias, out):
         table_warmer = consts.tile([P, 1], F32)
         nc.scalar.activation(out=table_warmer[:], in_=ones[:], func=ACT.Sqrt)
 
+        idle_sum = product_pool.tile([P, IDLE_COLS], F32, tag="product")
+        for k in range(IDLE_FIRST):
+            idle_pass(nc, idle_sum, zero_codes, zero_scales, k)
+
+        bias_words = bias_rows[:].bitcast(F32).rearrange("c (p v) -> c v p", v=2)
+        bias_turned = turned_pool.tile([P, 2, P], F32, tag="turned")
+        for v in range(2):
+            nc.tensor.transpose(bias_turned[:, v, :], bias_words[:, v, :], ident[:])
+
         groups = range(GROUPS)
-        centred = [centre(nc, acts, x_groups[g]) for g in groups]
+        centred = [
+            centre(nc, acts, x_groups[g][:].rearrange("q n c t s -> q n (c t) s"))
+            for g in groups
+        ]
         squared = [square(nc, acts, centred[g]) for g in groups]
+        bias_sb = consts.tile([P, CAPS, O_TILES], F32)
+        nc.scalar.copy(
+            out=bias_sb[:].rearrange("p c (v e) -> p c v e", v=2),
+            in_=bias_turned[:].bitcast(BF16).rearrange("p v (c e) -> p c v e", e=2)[:, 0:CAPS],
+        )
         grouped_0 = turn_weights(nc, caps, turned_pool, w_rows_all[0], ident)
-        std = [deviation(nc, acts, squared[g]) for g in groups]
+        idle_pass(nc, idle_sum, zero_codes, zero_scales, IDLE_FIRST)
+        sum_sq = [channel_sums(nc, acts, squared[g][:]) for g in groups]
+        std = [deviation(nc, acts, sum_sq[g]) for g in groups]
         w_mx = [quantise_weights(nc, caps, grouped_0)]
-        xn = [normalise(nc, acts, centred[g], std[g]) for g in groups]
+        rstd = [reciprocal(nc, acts, std[g]) for g in groups]
+        xn = [normalise(nc, acts, centred[g], rstd[g]) for g in groups]
         x_mx = [quantise_samples(nc, acts, xn[g]) for g in groups]
 
         out_view = out.rearrange(
@@ -220,7 +268,9 @@ def tile_caps_bn_s_kernel(tc, x, weight, bias, out):
             if c < CAPS:
                 grouped = turn_weights(nc, caps, turned_pool, w_rows_all[c], ident)
                 w_mx.append(quantise_weights(nc, caps, grouped))
-            if c >= LAG:
+            if c < LAG:
+                idle_pass(nc, idle_sum, zero_codes, zero_scales, IDLE_FIRST + c)
+            else:
                 m = c - LAG
                 multiply(
                     nc,

@@ -31,8 +31,6 @@ FLOPS = 2 * CAPS * D * D * SAMPLES
 
 
 LAG = 3
-IDLE_COLS = 512
-IDLE_FIRST = 12
 
 
 def channel_sums(nc, pool, values):
@@ -166,18 +164,6 @@ def multiply(nc, pool, product_pool, w_mx, x_mx, place, bias_c, out_c):
     nc.sync.dma_start(out=out_c, in_=result[:].rearrange("p n j s -> p n (j s)"))
 
 
-def idle_pass(nc, idle_sum, zero_codes, zero_scales, k):
-    nc.tensor.matmul_mx(
-        out=idle_sum[:],
-        lhsT=zero_codes[:, 0:P].bitcast(FP8X4),
-        lhsT_scale=zero_scales[:, 0:P],
-        rhs=zero_codes[:].bitcast(FP8X4),
-        rhs_scale=zero_scales[:],
-        start=(k == 0),
-        stop=(k == IDLE_FIRST + LAG - 1),
-    )
-
-
 def tile_caps_bn_s_kernel(tc, x, weight, bias, out):
     nc = tc.nc
     with ExitStack() as ctx:
@@ -218,23 +204,12 @@ def tile_caps_bn_s_kernel(tc, x, weight, bias, out):
         nc.scalar.dma_start(
             out=bias_rows[0:CAPS, :], in_=bias.rearrange("(c o) -> c o", c=CAPS)
         )
-        zeros = consts.tile([P, IDLE_COLS * PACK], BF16, align_bytes=64)
-        nc.vector.memset(zeros[:].bitcast(I32), 0)
-        zero_codes = consts.tile([P, IDLE_COLS], U32, align_bytes=64)
-        zero_scales = consts.tile([P, IDLE_COLS], U8, align_bytes=64)
-        nc.vector.quantize_mx(
-            out=zero_codes[:].bitcast(FP8X4), scales=zero_scales[:], in_=zeros[:]
-        )
         ident = consts.tile([P, P], F32)
         make_identity(nc, ident[:])
         ones = consts.tile([P, 1], F32)
         nc.vector.memset(ones[:], 1.0)
         table_warmer = consts.tile([P, 1], F32)
         nc.scalar.activation(out=table_warmer[:], in_=ones[:], func=ACT.Sqrt)
-
-        idle_sum = product_pool.tile([P, IDLE_COLS], F32, tag="product")
-        for k in range(IDLE_FIRST):
-            idle_pass(nc, idle_sum, zero_codes, zero_scales, k)
 
         bias_words = bias_rows[:].bitcast(F32).rearrange("c (p v) -> c v p", v=2)
         bias_turned = turned_pool.tile([P, 2, P], F32, tag="turned")
@@ -253,7 +228,6 @@ def tile_caps_bn_s_kernel(tc, x, weight, bias, out):
             in_=bias_turned[:].bitcast(BF16).rearrange("p v (c e) -> p c v e", e=2)[:, 0:CAPS],
         )
         grouped_0 = turn_weights(nc, caps, turned_pool, w_rows_all[0], ident)
-        idle_pass(nc, idle_sum, zero_codes, zero_scales, IDLE_FIRST)
         sum_sq = [channel_sums(nc, acts, squared[g][:]) for g in groups]
         std = [deviation(nc, acts, sum_sq[g]) for g in groups]
         w_mx = [quantise_weights(nc, caps, grouped_0)]
@@ -268,9 +242,7 @@ def tile_caps_bn_s_kernel(tc, x, weight, bias, out):
             if c < CAPS:
                 grouped = turn_weights(nc, caps, turned_pool, w_rows_all[c], ident)
                 w_mx.append(quantise_weights(nc, caps, grouped))
-            if c < LAG:
-                idle_pass(nc, idle_sum, zero_codes, zero_scales, IDLE_FIRST + c)
-            else:
+            if c >= LAG:
                 m = c - LAG
                 multiply(
                     nc,

@@ -30,36 +30,41 @@ BANK_TILES = 2
 FLOPS = 2 * CAPS * D * D * SAMPLES
 
 
+LAST_TILES = 1
 LAG = 3
 
 
-def channel_sums(nc, pool, values):
-    sums = pool.tile([P, GROUP_CH], F32)
-    nc.vector.tensor_reduce(
-        out=sums[:], in_=values.rearrange("q n k s -> q k n s"), axis=AXIS.XY, op=ALU.add
-    )
-    return sums
-
-
-def over_samples(per_channel):
-    return per_channel[:].unsqueeze(1).unsqueeze(3).to_broadcast([P, BATCH, GROUP_CH, HW])
-
-
-def centre(nc, pool, x_values):
-    total = channel_sums(nc, pool, x_values)
+def centre(nc, pool, x_group):
+    x_by_channel = x_group[:].rearrange("q n c t s -> q (c t) n s")
+    total = pool.tile([P, GROUP_CH], F32)
+    nc.vector.tensor_reduce(out=total[:], in_=x_by_channel, axis=AXIS.XY, op=ALU.add)
     neg_mean = pool.tile([P, GROUP_CH], F32)
     nc.vector.tensor_scalar_mul(out=neg_mean[:], in0=total[:], scalar1=-1.0 / SAMPLES)
-    centred = pool.tile([P, BATCH, GROUP_CH, HW], F32)
+    centred = pool.tile([P, GROUP_CH, BATCH, HW], F32)
     nc.vector.tensor_tensor(
-        out=centred[:], in0=x_values, in1=over_samples(neg_mean), op=ALU.add
+        out=centred[:],
+        in0=x_by_channel,
+        in1=neg_mean[:].unsqueeze(2).unsqueeze(3).to_broadcast([P, GROUP_CH, BATCH, HW]),
+        op=ALU.add,
     )
     return centred
 
 
 def square(nc, pool, centred):
-    squared = pool.tile([P, BATCH, GROUP_CH, HW], F32)
+    squared = pool.tile([P, GROUP_CH, BATCH, HW], F32)
     nc.scalar.activation(out=squared[:], in_=centred[:], func=ACT.Square)
     return squared
+
+
+def sum_squares(nc, pool, squared):
+    sum_sq = pool.tile([P, GROUP_CH], F32)
+    nc.vector.tensor_reduce(
+        out=sum_sq[:],
+        in_=squared[:].rearrange("q k n s -> q k (n s)"),
+        axis=AXIS.X,
+        op=ALU.add,
+    )
+    return sum_sq
 
 
 def deviation(nc, pool, sum_sq):
@@ -84,17 +89,16 @@ def reciprocal(nc, pool, std):
 
 
 def normalise(nc, pool, centred, rstd):
-    xn = pool.tile([P, BATCH, GROUP_CAPS, HW, PACK], BF16, align_bytes=64)
-    for n in range(BATCH):
-        nc.vector.tensor_tensor(
-            out=xn[:, n],
-            in0=centred[:, n].rearrange("q (c t) s -> q c s t", t=PACK),
-            in1=rstd[:]
-            .rearrange("q (c t) -> q c t", t=PACK)
-            .unsqueeze(2)
-            .to_broadcast([P, GROUP_CAPS, HW, PACK]),
-            op=ALU.mult,
-        )
+    xn = pool.tile([P, GROUP_CAPS, SAMPLES, PACK], BF16, align_bytes=64)
+    nc.vector.tensor_tensor(
+        out=xn[:],
+        in0=centred[:].rearrange("q (c t) n s -> q c (n s) t", t=PACK),
+        in1=rstd[:]
+        .rearrange("q (c t) -> q c t", t=PACK)
+        .unsqueeze(2)
+        .to_broadcast([P, GROUP_CAPS, SAMPLES, PACK]),
+        op=ALU.mult,
+    )
     return xn
 
 
@@ -104,38 +108,38 @@ def quantise_samples(nc, pool, xn):
     nc.vector.quantize_mx(
         out=x_codes[:].bitcast(FP8X4),
         scales=x_scales[:],
-        in_=xn[:].rearrange("q n c s t -> q (n c s t)"),
+        in_=xn[:].rearrange("q c m t -> q (c m t)"),
     )
     return x_codes, x_scales
 
 
-def turn_weights(nc, pool, turned_pool, w_rows, ident):
+def turn_weights(nc, pool, turned_pool, w_rows, ident, tiles):
     w_words = w_rows[:].bitcast(F32)
     grouped = pool.tile([P, O_TILES, P, PACK], BF16, align_bytes=64)
     grouped_words = grouped[:].bitcast(F32)
-    for j0 in range(0, O_TILES, BANK_TILES):
-        turned = turned_pool.tile([P, BANK_TILES, 2, P], F32)
-        for jj in range(BANK_TILES):
+    for j0 in range(0, O_TILES, tiles):
+        turned = turned_pool.tile([P, tiles, 2, P], F32)
+        for jj in range(tiles):
             for u in range(2):
                 nc.tensor.transpose(
                     turned[:, jj, u, :], w_words[:, j0 + jj, u * P : (u + 1) * P], ident[:]
                 )
         nc.scalar.copy(
-            out=grouped_words[:, j0 : j0 + BANK_TILES],
+            out=grouped_words[:, j0 : j0 + tiles],
             in_=turned[:].rearrange("q j u r -> q j r u"),
         )
     return grouped
 
 
-def quantise_weights(nc, pool, grouped):
+def quantise_weights(nc, pool, grouped, tiles):
     w_codes = pool.tile([P, O_TILES * P], U32, align_bytes=64)
     w_scales = pool.tile([P, O_TILES * P], U8, align_bytes=64)
-    for j0 in range(0, O_TILES, BANK_TILES):
-        cols = slice(j0 * P, (j0 + BANK_TILES) * P)
+    for j0 in range(0, O_TILES, tiles):
+        cols = slice(j0 * P, (j0 + tiles) * P)
         nc.vector.quantize_mx(
             out=w_codes[:, cols].bitcast(FP8X4),
             scales=w_scales[:, cols],
-            in_=grouped[:, j0 : j0 + BANK_TILES].rearrange("q j r t -> q (j r t)"),
+            in_=grouped[:, j0 : j0 + tiles].rearrange("q j r t -> q (j r t)"),
         )
     return w_codes, w_scales
 
@@ -157,7 +161,9 @@ def multiply(nc, pool, product_pool, w_mx, x_mx, place, bias_c, out_c):
     result = pool.tile([P, BATCH, O_TILES, HW], F32)
     nc.vector.tensor_tensor(
         out=result[:],
-        in0=product[:].rearrange("p j (n c s) -> p c n j s", n=BATCH, c=GROUP_CAPS)[:, place],
+        in0=product[:, :, place * SAMPLES : (place + 1) * SAMPLES].rearrange(
+            "p j (n s) -> p n j s", n=BATCH
+        ),
         in1=bias_c.unsqueeze(1).unsqueeze(3).to_broadcast([P, BATCH, O_TILES, HW]),
         op=ALU.add,
     )
@@ -193,9 +199,9 @@ def tile_caps_bn_s_kernel(tc, x, weight, bias, out):
             if c < CAPS - 1:
                 nc.sync.dma_start(out=w_rows[:], in_=w_view)
             else:
-                for j0 in range(0, O_TILES, BANK_TILES):
+                for j0 in range(0, O_TILES, LAST_TILES):
                     nc.sync.dma_start(
-                        out=w_rows[:, j0 : j0 + BANK_TILES], in_=w_view[:, j0 : j0 + BANK_TILES]
+                        out=w_rows[:, j0 : j0 + LAST_TILES], in_=w_view[:, j0 : j0 + LAST_TILES]
                     )
             w_rows_all.append(w_rows)
 
@@ -217,20 +223,17 @@ def tile_caps_bn_s_kernel(tc, x, weight, bias, out):
             nc.tensor.transpose(bias_turned[:, v, :], bias_words[:, v, :], ident[:])
 
         groups = range(GROUPS)
-        centred = [
-            centre(nc, acts, x_groups[g][:].rearrange("q n c t s -> q n (c t) s"))
-            for g in groups
-        ]
+        centred = [centre(nc, acts, x_groups[g]) for g in groups]
         squared = [square(nc, acts, centred[g]) for g in groups]
         bias_sb = consts.tile([P, CAPS, O_TILES], F32)
         nc.scalar.copy(
             out=bias_sb[:].rearrange("p c (v e) -> p c v e", v=2),
             in_=bias_turned[:].bitcast(BF16).rearrange("p v (c e) -> p c v e", e=2)[:, 0:CAPS],
         )
-        grouped_0 = turn_weights(nc, caps, turned_pool, w_rows_all[0], ident)
-        sum_sq = [channel_sums(nc, acts, squared[g][:]) for g in groups]
+        grouped_0 = turn_weights(nc, caps, turned_pool, w_rows_all[0], ident, BANK_TILES)
+        sum_sq = [sum_squares(nc, acts, squared[g]) for g in groups]
         std = [deviation(nc, acts, sum_sq[g]) for g in groups]
-        w_mx = [quantise_weights(nc, caps, grouped_0)]
+        w_mx = [quantise_weights(nc, caps, grouped_0, BANK_TILES)]
         rstd = [reciprocal(nc, acts, std[g]) for g in groups]
         xn = [normalise(nc, acts, centred[g], rstd[g]) for g in groups]
         x_mx = [quantise_samples(nc, acts, xn[g]) for g in groups]
@@ -240,8 +243,9 @@ def tile_caps_bn_s_kernel(tc, x, weight, bias, out):
         )
         for c in range(1, CAPS + LAG):
             if c < CAPS:
-                grouped = turn_weights(nc, caps, turned_pool, w_rows_all[c], ident)
-                w_mx.append(quantise_weights(nc, caps, grouped))
+                tiles = BANK_TILES if c < CAPS - 1 else LAST_TILES
+                grouped = turn_weights(nc, caps, turned_pool, w_rows_all[c], ident, tiles)
+                w_mx.append(quantise_weights(nc, caps, grouped, tiles))
             if c >= LAG:
                 m = c - LAG
                 multiply(

from contextlib import ExitStack

import concourse.mybir as mybir
from concourse.masks import make_identity

F32 = mybir.dt.float32
BF16 = mybir.dt.bfloat16
U32 = mybir.dt.uint32
U8 = mybir.dt.uint8
I32 = mybir.dt.int32
FP8X4 = mybir.dt.float8_e4m3fn_x4
ALU = mybir.AluOpType
ACT = mybir.ActivationFunctionType
AXIS = mybir.AxisListType

P = 128
PACK = 4
BATCH = 2
CAPS = 8
D = 512
HW = 16
EPS = 1e-5
SAMPLES = BATCH * HW
O_TILES = D // P
GROUPS = 2
GROUP_CAPS = CAPS // GROUPS
GROUP_CH = GROUP_CAPS * PACK
BANK_TILES = 2

FLOPS = 2 * CAPS * D * D * SAMPLES


LAST_TILES = 1
LAG = 3


def centre(nc, pool, x_group):
    x_by_channel = x_group[:].rearrange("q n c t s -> q (c t) n s")
    total = pool.tile([P, GROUP_CH], F32)
    nc.vector.tensor_reduce(out=total[:], in_=x_by_channel, axis=AXIS.XY, op=ALU.add)
    neg_mean = pool.tile([P, GROUP_CH], F32)
    nc.vector.tensor_scalar_mul(out=neg_mean[:], in0=total[:], scalar1=-1.0 / SAMPLES)
    centred = pool.tile([P, GROUP_CH, BATCH, HW], F32)
    nc.vector.tensor_tensor(
        out=centred[:],
        in0=x_by_channel,
        in1=neg_mean[:].unsqueeze(2).unsqueeze(3).to_broadcast([P, GROUP_CH, BATCH, HW]),
        op=ALU.add,
    )
    return centred


def square(nc, pool, centred):
    squared = pool.tile([P, GROUP_CH, BATCH, HW], F32)
    nc.scalar.activation(out=squared[:], in_=centred[:], func=ACT.Square)
    return squared


def sum_squares(nc, pool, squared):
    sum_sq = pool.tile([P, GROUP_CH], F32)
    nc.vector.tensor_reduce(
        out=sum_sq[:],
        in_=squared[:].rearrange("q k n s -> q k (n s)"),
        axis=AXIS.X,
        op=ALU.add,
    )
    return sum_sq


def deviation(nc, pool, sum_sq):
    var_eps = pool.tile([P, GROUP_CH], F32)
    nc.vector.tensor_scalar(
        out=var_eps[:],
        in0=sum_sq[:],
        scalar1=1.0 / SAMPLES,
        scalar2=EPS,
        op0=ALU.mult,
        op1=ALU.add,
    )
    std = pool.tile([P, GROUP_CH], F32)
    nc.scalar.activation(out=std[:], in_=var_eps[:], func=ACT.Sqrt)
    return std


def reciprocal(nc, pool, std):
    rstd = pool.tile([P, GROUP_CH], F32)
    nc.vector.reciprocal(out=rstd[:], in_=std[:])
    return rstd


def normalise(nc, pool, centred, rstd):
    xn = pool.tile([P, GROUP_CAPS, SAMPLES, PACK], BF16, align_bytes=64)
    nc.vector.tensor_tensor(
        out=xn[:],
        in0=centred[:].rearrange("q (c t) n s -> q c (n s) t", t=PACK),
        in1=rstd[:]
        .rearrange("q (c t) -> q c t", t=PACK)
        .unsqueeze(2)
        .to_broadcast([P, GROUP_CAPS, SAMPLES, PACK]),
        op=ALU.mult,
    )
    return xn


def quantise_samples(nc, pool, xn):
    x_codes = pool.tile([P, GROUP_CAPS * SAMPLES], U32, align_bytes=64)
    x_scales = pool.tile([P, GROUP_CAPS * SAMPLES], U8, align_bytes=64)
    nc.vector.quantize_mx(
        out=x_codes[:].bitcast(FP8X4),
        scales=x_scales[:],
        in_=xn[:].rearrange("q c m t -> q (c m t)"),
    )
    return x_codes, x_scales


def turn_weights(nc, pool, turned_pool, w_rows, ident, tiles):
    w_words = w_rows[:].bitcast(F32)
    grouped = pool.tile([P, O_TILES, P, PACK], BF16, align_bytes=64)
    grouped_words = grouped[:].bitcast(F32)
    for j0 in range(0, O_TILES, tiles):
        turned = turned_pool.tile([P, tiles, 2, P], F32)
        for jj in range(tiles):
            for u in range(2):
                nc.tensor.transpose(
                    turned[:, jj, u, :], w_words[:, j0 + jj, u * P : (u + 1) * P], ident[:]
                )
        nc.scalar.copy(
            out=grouped_words[:, j0 : j0 + tiles],
            in_=turned[:].rearrange("q j u r -> q j r u"),
        )
    return grouped


def quantise_weights(nc, pool, grouped, tiles):
    w_codes = pool.tile([P, O_TILES * P], U32, align_bytes=64)
    w_scales = pool.tile([P, O_TILES * P], U8, align_bytes=64)
    for j0 in range(0, O_TILES, tiles):
        cols = slice(j0 * P, (j0 + tiles) * P)
        nc.vector.quantize_mx(
            out=w_codes[:, cols].bitcast(FP8X4),
            scales=w_scales[:, cols],
            in_=grouped[:, j0 : j0 + tiles].rearrange("q j r t -> q (j r t)"),
        )
    return w_codes, w_scales


def multiply(nc, pool, product_pool, w_mx, x_mx, place, bias_c, out_c):
    w_codes, w_scales = w_mx
    x_codes, x_scales = x_mx
    product = product_pool.tile([P, O_TILES, GROUP_CAPS * SAMPLES], F32)
    for j in range(O_TILES):
        nc.tensor.matmul_mx(
            out=product[:, j, :],
            lhsT=w_codes[:, j * P : (j + 1) * P].bitcast(FP8X4),
            lhsT_scale=w_scales[:, j * P : (j + 1) * P],
            rhs=x_codes[:].bitcast(FP8X4),
            rhs_scale=x_scales[:],
            start=True,
            stop=True,
        )
    result = pool.tile([P, BATCH, O_TILES, HW], F32)
    nc.vector.tensor_tensor(
        out=result[:],
        in0=product[:, :, place * SAMPLES : (place + 1) * SAMPLES].rearrange(
            "p j (n s) -> p n j s", n=BATCH
        ),
        in1=bias_c.unsqueeze(1).unsqueeze(3).to_broadcast([P, BATCH, O_TILES, HW]),
        op=ALU.add,
    )
    nc.sync.dma_start(out=out_c, in_=result[:].rearrange("p n j s -> p n (j s)"))


def tile_caps_bn_s_kernel(tc, x, weight, bias, out):
    nc = tc.nc
    with ExitStack() as ctx:
        consts = ctx.enter_context(tc.tile_pool(name="consts", bufs=1))
        acts = ctx.enter_context(tc.tile_pool(name="acts", bufs=GROUPS))
        caps = ctx.enter_context(tc.tile_pool(name="caps", bufs=CAPS))
        turned_pool = ctx.enter_context(tc.psum_pool(name="turned", bufs=6))
        product_pool = ctx.enter_context(tc.psum_pool(name="product", bufs=2))
        ctx.enter_context(tc.manual_schedule())

        x_view = x.rearrange(
            "n (c u q e) h w -> q n c u (e h w)", c=CAPS, u=2, q=P, e=2
        )
        x_groups = []
        for g in range(GROUPS):
            x_group = acts.tile([P, BATCH, GROUP_CAPS, PACK, HW], BF16)
            for n in range(BATCH):
                nc.sync.dma_start(
                    out=x_group[:, n].rearrange("q c (u e) s -> q c u (e s)", u=2),
                    in_=x_view[:, n, g * GROUP_CAPS : (g + 1) * GROUP_CAPS],
                )
            x_groups.append(x_group)
        w_rows_all = []
        for c in range(CAPS):
            w_rows = caps.tile([P, O_TILES, D], BF16)
            w_view = weight[c].rearrange("(p j) i -> p j i", j=O_TILES)
            if c < CAPS - 1:
                nc.sync.dma_start(out=w_rows[:], in_=w_view)
            else:
                for j0 in range(0, O_TILES, LAST_TILES):
                    nc.sync.dma_start(
                        out=w_rows[:, j0 : j0 + LAST_TILES], in_=w_view[:, j0 : j0 + LAST_TILES]
                    )
            w_rows_all.append(w_rows)

        bias_rows = consts.tile([P, D], BF16)
        nc.vector.memset(bias_rows[:].bitcast(I32), 0)
        nc.scalar.dma_start(
            out=bias_rows[0:CAPS, :], in_=bias.rearrange("(c o) -> c o", c=CAPS)
        )
        ident = consts.tile([P, P], F32)
        make_identity(nc, ident[:])
        ones = consts.tile([P, 1], F32)
        nc.vector.memset(ones[:], 1.0)
        table_warmer = consts.tile([P, 1], F32)
        nc.scalar.activation(out=table_warmer[:], in_=ones[:], func=ACT.Sqrt)

        bias_words = bias_rows[:].bitcast(F32).rearrange("c (p v) -> c v p", v=2)
        bias_turned = turned_pool.tile([P, 2, P], F32, tag="turned")
        for v in range(2):
            nc.tensor.transpose(bias_turned[:, v, :], bias_words[:, v, :], ident[:])

        groups = range(GROUPS)
        centred = [centre(nc, acts, x_groups[g]) for g in groups]
        squared = [square(nc, acts, centred[g]) for g in groups]
        bias_sb = consts.tile([P, CAPS, O_TILES], F32)
        nc.scalar.copy(
            out=bias_sb[:].rearrange("p c (v e) -> p c v e", v=2),
            in_=bias_turned[:].bitcast(BF16).rearrange("p v (c e) -> p c v e", e=2)[:, 0:CAPS],
        )
        grouped_0 = turn_weights(nc, caps, turned_pool, w_rows_all[0], ident, BANK_TILES)
        sum_sq = [sum_squares(nc, acts, squared[g]) for g in groups]
        std = [deviation(nc, acts, sum_sq[g]) for g in groups]
        w_mx = [quantise_weights(nc, caps, grouped_0, BANK_TILES)]
        rstd = [reciprocal(nc, acts, std[g]) for g in groups]
        xn = [normalise(nc, acts, centred[g], rstd[g]) for g in groups]
        x_mx = [quantise_samples(nc, acts, xn[g]) for g in groups]

        out_view = out.rearrange(
            "n (c p j) h w -> c p n (j h w)", c=CAPS, p=P, j=O_TILES
        )
        for c in range(1, CAPS + LAG):
            if c < CAPS:
                tiles = BANK_TILES if c < CAPS - 1 else LAST_TILES
                grouped = turn_weights(nc, caps, turned_pool, w_rows_all[c], ident, tiles)
                w_mx.append(quantise_weights(nc, caps, grouped, tiles))
            if c >= LAG:
                m = c - LAG
                multiply(
                    nc,
                    caps,
                    product_pool,
                    w_mx[m],
                    x_mx[m // GROUP_CAPS],
                    m % GROUP_CAPS,
                    bias_sb[:, m, :],
                    out_view[m],
                )
